import numpy as np
import ml_dtypes


def mxq(x, axis, fmt="e4m3"):
    dtype, down = {"e4m3": (ml_dtypes.float8_e4m3fn, 7), "e5m2": (ml_dtypes.float8_e5m2, 14)}[fmt]
    v = np.moveaxis(np.asarray(x, np.float32).astype(ml_dtypes.bfloat16).astype(np.float64), axis, -1)
    blocks = v.reshape(v.shape[:-1] + (-1, 32))
    amax = np.abs(blocks).max(-1, keepdims=True)
    byte = np.maximum(np.where(amax > 0, np.frexp(amax)[1] - 1 + 127, 0) - down, 1)
    scale = np.exp2(byte - 127.0)
    codes = (blocks / scale).astype(np.float32).astype(dtype).astype(np.float64)
    return np.moveaxis((codes * scale).reshape(v.shape), -1, axis)


WIDE = False


def mx_kscale(k):
    if not WIDE:
        return np.ones(k)
    levels = np.array([10, -10, 5, -5, 0])
    a = np.random.permutation(np.resize(levels, k // 512 * 4)).reshape(k // 512, 4)
    idx = np.arange(k)
    return np.exp2(a[idx // 512, idx % 128 // 32])


BF16 = ml_dtypes.bfloat16


def bf(x):
    return np.asarray(x, np.float32).astype(BF16)


def f64(x):
    return np.asarray(x).astype(np.float64)


B, T, C, CO, HS, DW, DA, DV, DG = 4, 128, 2048, 2048, 64, 128, 128, 128, 256


def sigmoid(u):
    return 1.0 / (1.0 + np.exp(-u))


def setup_inputs():
    n = np.random.standard_normal
    s = mx_kscale(C)
    return {
        "x": bf(n((B, T, C)) * s),
        "x_v": bf(n((1, 1, C)) * 0.3),
        "W_v": bf(n((CO, C)) / np.sqrt(C) / s),
        "v_hid": bf(n((B, T, DV))),
        "v2": bf(n((DV, CO)) / np.sqrt(DV)),
        "v0": bf(0.73 + n((1, 1, CO)) * 0.2),
        "v_first": bf(n((B, T, CO))),
    }


def reference(x, x_v, W_v, v_hid, v2, v0, v_first):
    x = f64(x)
    prev = np.concatenate([np.zeros_like(x[:, :1]), x[:, :-1]], axis=1)
    xv = x + (prev - x) * f64(x_v)
    v = mxq(xv, 2, "e4m3") @ mxq(f64(W_v), 1, "e4m3").T
    mix = sigmoid(f64(v0) + f64(v_hid) @ f64(v2))
    return v + (f64(v_first) - v) * mix

@@ -1,0 +1,244 @@
+from contextlib import ExitStack
+
+import concourse.bass as bass
+import concourse.mybir as mybir
+import concourse.tile as tile
+from concourse.masks import make_identity
+
+F32 = mybir.dt.float32
+BF16 = mybir.dt.bfloat16
+U32 = mybir.dt.uint32
+U8 = mybir.dt.uint8
+FP8X4 = mybir.dt.float8_e4m3fn_x4
+ALU = mybir.AluOpType
+ACT = mybir.ActivationFunctionType
+
+P = 128
+NB = 4
+C = 2048
+CO = 2048
+NG = 4
+UW = 256
+NU = CO // UW
+CW = 512
+NCH = CO // CW
+
+FLOPS = 2 * NB * P * C * CO + 2 * NB * P * 128 * CO
+
+
+def tile_full_tmix_params_pb_kernel(tc, x, x_v, W_v, v_hid, v2, v0, v_first, out):
+    nc = tc.nc
+    with ExitStack() as ctx:
+        const = ctx.enter_context(tc.tile_pool(name="const", bufs=1))
+        wraw_pool = ctx.enter_context(tc.tile_pool(name="wraw", bufs=5))
+        wg_pool = ctx.enter_context(tc.tile_pool(name="wg", bufs=2))
+        wc_pool = ctx.enter_context(tc.tile_pool(name="wc", bufs=4))
+        xw_pool = ctx.enter_context(tc.tile_pool(name="xw", bufs=2))
+        vf_pool = ctx.enter_context(tc.tile_pool(name="vf", bufs=3))
+        p_pool = ctx.enter_context(tc.tile_pool(name="pp", bufs=4))
+        acc_pool = ctx.enter_context(tc.psum_pool(name="acc", bufs=4))
+        tp_pool = ctx.enter_context(tc.psum_pool(name="tp", bufs=4))
+
+        ident_f = const.tile([P, P], F32, name="ident_f")
+        make_identity(nc, ident_f[:])
+        ident_b = const.tile([P, P], BF16, name="ident_b")
+        make_identity(nc, ident_b[:])
+
+        a_bf = const.tile([P, 8, 2], BF16, name="a_bf")
+        nc.scalar.dma_start(out=a_bf[:], in_=x_v.rearrange("a b c -> (a b c)").rearrange("(m p e) -> p m e", p=P, e=2))
+
+        x_sb = []
+        for b in range(NB):
+            xt = const.tile([P, C], BF16, name="x_sb%d" % b)
+            nc.sync.dma_start(out=xt[:], in_=x[b])
+            x_sb.append(xt)
+        vh_sb = const.tile([P, NB, P], BF16, name="vh_sb")
+        nc.sync.dma_start(out=vh_sb[:], in_=v_hid.rearrange("b t d -> t b d"))
+        v2_sb = const.tile([P, CO], BF16, name="v2_sb")
+        nc.sync.dma_start(out=v2_sb[:], in_=v2)
+        v0b = const.tile([P, CO], BF16, name="v0b")
+        nc.sync.dma_start(out=v0b[:], in_=v0.rearrange("a b c -> (a b c)").partition_broadcast(P))
+
+        w_units = W_v.rearrange("(n r p) k -> n p r k", r=2, p=P)
+        vf_chunks = v_first.rearrange("b t (c n) -> c t b n", n=CW)
+        wraw = []
+        vf_sb = []
+        for n in range(NU):
+            wr = wraw_pool.tile([P, 2, C], BF16, name="wr")
+            nc.sync.dma_start(out=wr[:], in_=w_units[n])
+            wraw.append(wr)
+            if n % 2 == 1:
+                vf = vf_pool.tile([P, NB, CW], BF16, name="vf")
+                nc.sync.dma_start(out=vf[:], in_=vf_chunks[n // 2])
+                vf_sb.append(vf)
+
+        a32 = const.tile([P, 16], F32, name="a32")
+        nc.vector.tensor_copy(out=a32[:], in_=a_bf[:].rearrange("p m e -> p (m e)"))
+        oma32 = const.tile([P, 16], F32, name="oma32")
+        nc.vector.tensor_scalar(out=oma32[:], in0=a32[:], scalar1=-1.0, scalar2=1.0, op0=ALU.mult, op1=ALU.add)
+
+        xcodes = []
+        xscales = []
+        for b in range(NB):
+            xcodes.append(const.tile([P, NG * P], U32, name="xcodes%d" % b, align_bytes=64))
+            xscales.append(const.tile([P, NG * P], U8, name="xscales%d" % b, align_bytes=64))
+        mix = {}
+        t1 = {}
+        for c in range(NCH):
+            for i in range(NB):
+                mix[(c, i)] = const.tile([P, CW], F32, name="mix%d_%d" % (c, i))
+                t1[(c, i)] = const.tile([P, CW], F32, name="t1_%d_%d" % (c, i))
+        vhT = const.tile([P, NB * P], BF16, name="vhT")
+
+        xbanks = {}
+        xvps = {}
+        xgs = {}
+
+        def x_transposes(b):
+            xwords = x_sb[b][:].bitcast(F32)
+            banks = []
+            for hb in range(2):
+                bank = tp_pool.tile([P, 512], F32, name="xbank", tag="tp")
+                for q in range(4):
+                    m = 4 * hb + q
+                    nc.tensor.transpose(bank[:, P * q:P * q + P], xwords[:, P * m:P * m + P], ident_f[:])
+                banks.append(bank)
+            xbanks[b] = banks
+
+        def x_mix(b):
+            y0 = xw_pool.tile([P, 16, P], F32, name="y0")
+            xvp = xw_pool.tile([P, 16, P], BF16, name="xvp")
+            for hb in range(2):
+                view = xbanks[b][hb][:].bitcast(BF16).rearrange("p (q s e) -> p q s e", q=4, e=2)
+                for q in range(4):
+                    for e in range(2):
+                        j = 8 * hb + 2 * q + e
+                        nc.scalar.activation(out=y0[:, j, :], in_=view[:, q, :, e], func=ACT.Copy,
+                                             scale=oma32[:, j:j + 1])
+                for q in range(4):
+                    for e in range(2):
+                        j = 8 * hb + 2 * q + e
+                        nc.vector.scalar_tensor_tensor(out=xvp[:, j, 1:P], in0=view[:, q, 0:P - 1, e],
+                                                       scalar=a32[:, j:j + 1], in1=y0[:, j, 1:P],
+                                                       op0=ALU.mult, op1=ALU.add)
+            nc.vector.tensor_copy(out=xvp[:, :, 0:1], in_=y0[:, :, 0:1])
+            xvps[b] = xvp
+
+        def x_regroup(b):
+            xg = xw_pool.tile([P, NG * P * 4], BF16, name="xg", align_bytes=64)
+            nc.vector.tensor_copy(out=xg[:].rearrange("p (g s t) -> p g s t", g=NG, t=4),
+                                  in_=xvps[b][:].rearrange("p (g t) s -> p g s t", t=4))
+            xgs[b] = xg
+
+        def x_quant(b):
+            nc.vector.quantize_mx(out=xcodes[b][:].bitcast(FP8X4), scales=xscales[b][:], in_=xgs[b][:])
+
+        def vh_transposes():
+            bank = tp_pool.tile([P, NB * P], BF16, name="vhbank", tag="tp")
+            for b in range(NB):
+                nc.tensor.transpose(bank[:, P * b:P * b + P], vh_sb[:, b, :], ident_b[:])
+            nc.scalar.copy(out=vhT[:], in_=bank[:])
+
+        def gate(c):
+            cols = slice(CW * c, CW * c + CW)
+            for i in range(NB):
+                hp = tp_pool.tile([P, CW], F32, name="hp", tag="tp")
+                nc.tensor.matmul(out=hp[:], lhsT=vhT[:, P * i:P * i + P], rhs=v2_sb[:, cols], start=True, stop=True)
+                nc.vector.tensor_tensor(out=t1[(c, i)][:], in0=hp[:], in1=v0b[:, cols], op=ALU.add)
+                nc.scalar.activation(out=mix[(c, i)][:], in_=t1[(c, i)][:], func=ACT.Sigmoid)
+                nc.gpsimd.tensor_tensor(out=t1[(c, i)][:], in0=vf_sb[c][:, i, :], in1=mix[(c, i)][:], op=ALU.mult)
+
+        wgs = {}
+        wcs = {}
+
+        def w_transposes(n):
+            wg = wg_pool.tile([P, NG * UW * 4], BF16, name="wg", align_bytes=64)
+            wgw = wg[:].bitcast(F32)
+            for g in range(NG):
+                bank = tp_pool.tile([P, 512], F32, name="wbank", tag="tp")
+                for u in range(2):
+                    for r in range(2):
+                        nc.tensor.transpose(bank[:, UW * u + P * r:UW * u + P * r + P],
+                                            wraw[n][:, r, :].bitcast(F32)[:, 256 * g + P * u:256 * g + P * u + P],
+                                            ident_f[:])
+                nc.scalar.copy(out=wgw[:, 512 * g:512 * g + 512].rearrange("p (c u) -> p c u", u=2),
+                               in_=bank[:].rearrange("p (u c) -> p c u", u=2))
+            wgs[n] = wg
+
+        def w_quant(n):
+            wc = wc_pool.tile([P, NG * UW], U32, name="wc", align_bytes=64)
+            ws = wc_pool.tile([P, NG * UW], U8, name="ws", align_bytes=64)
+            nc.vector.quantize_mx(out=wc[:].bitcast(FP8X4), scales=ws[:], in_=wgs[n][:])
+            wcs[n] = (wc, ws)
+
+        accs = {}
+
+        def mx(n, i):
+            c = n // 2
+            h = n % 2
+            if h == 0:
+                accs[(c, i)] = acc_pool.tile([P, CW], F32, name="acc", tag="acc")
+            acc = accs[(c, i)]
+            wc, ws = wcs[n]
+            for g in range(NG):
+                nc.tensor.matmul_mx(out=acc[:, UW * h:UW * h + UW],
+                                    lhsT=xcodes[i][:, P * g:P * g + P].bitcast(FP8X4),
+                                    lhsT_scale=xscales[i][:, P * g:P * g + P],
+                                    rhs=wc[:, UW * g:UW * g + UW].bitcast(FP8X4),
+                                    rhs_scale=ws[:, UW * g:UW * g + UW],
+                                    start=(g == 0), stop=(g == NG - 1))
+
+        def epilogue(c, i):
+            pt = p_pool.tile([P, CW], F32, name="pt")
+            nc.vector.scalar_tensor_tensor(out=pt[:], in0=mix[(c, i)][:], scalar=1.0, in1=accs[(c, i)][:],
+                                           op0=ALU.subtract, op1=ALU.mult)
+            nc.gpsimd.tensor_tensor(out=t1[(c, i)][:], in0=t1[(c, i)][:], in1=pt[:], op=ALU.subtract)
+            nc.sync.dma_start(out=out[i, :, CW * c:CW * c + CW], in_=t1[(c, i)][:])
+
+        x_transposes(0)
+        vh_transposes()
+        x_mix(0)
+        x_transposes(1)
+        x_regroup(0)
+        x_mix(1)
+        x_quant(0)
+        x_transposes(2)
+        x_regroup(1)
+        gate(0)
+        w_transposes(0)
+        x_mix(2)
+        x_quant(1)
+        x_transposes(3)
+        x_regroup(2)
+        w_quant(0)
+        mx(0, 0)
+        mx(0, 1)
+        w_transposes(1)
+        x_mix(3)
+        x_quant(2)
+        x_regroup(3)
+        w_quant(1)
+        x_quant(3)
+        mx(1, 0)
+        mx(1, 1)
+        epilogue(0, 0)
+        epilogue(0, 1)
+        mx(0, 2)
+        mx(1, 2)
+        epilogue(0, 2)
+        w_transposes(2)
+        mx(0, 3)
+        mx(1, 3)
+        epilogue(0, 3)
+        for c in range(1, NCH):
+            gate(c)
+            w_quant(2 * c)
+            w_transposes(2 * c + 1)
+            for i in range(NB):
+                mx(2 * c, i)
+            w_quant(2 * c + 1)
+            if c + 1 < NCH:
+                w_transposes(2 * c + 2)
+            for i in range(NB):
+                mx(2 * c + 1, i)
+                epilogue(c, i)

@@ -56,8 +56,10 @@ def tile_full_tmix_params_pb_kernel(tc, x, x_v, W_v, v_hid, v2, v0, v_first, out
         nc.sync.dma_start(out=vh_sb[:], in_=v_hid.rearrange("b t d -> t b d"))
         v2_sb = const.tile([P, CO], BF16, name="v2_sb")
         nc.sync.dma_start(out=v2_sb[:], in_=v2)
-        v0b = const.tile([P, CO], BF16, name="v0b")
-        nc.sync.dma_start(out=v0b[:], in_=v0.rearrange("a b c -> (a b c)").partition_broadcast(P))
+        v0rows = const.tile([P, P], BF16, name="v0rows")
+        nc.gpsimd.memset(v0rows[:], 0.0)
+        nc.sync.dma_start(out=v0rows[0:16, :], in_=v0.rearrange("a b c -> (a b c)").rearrange("(j p) -> j p", p=P))
+        v0c = const.tile([P, 16], F32, name="v0c")
 
         w_units = W_v.rearrange("(n r p) k -> n p r k", r=2, p=P)
         vf_chunks = v_first.rearrange("b t (c n) -> c t b n", n=CW)
@@ -126,8 +128,9 @@ def tile_full_tmix_params_pb_kernel(tc, x, x_v, W_v, v_hid, v2, v0, v_first, out
 
         def x_regroup(b):
             xg = xw_pool.tile([P, NG * P * 4], BF16, name="xg", align_bytes=64)
-            nc.vector.tensor_copy(out=xg[:].rearrange("p (g s t) -> p g s t", g=NG, t=4),
-                                  in_=xvps[b][:].rearrange("p (g t) s -> p g s t", t=4))
+            nc.gpsimd.tensor_scalar(out=xg[:].rearrange("p (g s t) -> p g s t", g=NG, t=4),
+                                    in0=xvps[b][:].rearrange("p (g t) s -> p g s t", t=4),
+                                    scalar1=1.0, scalar2=0.0, op0=ALU.mult, op1=ALU.add)
             xgs[b] = xg
 
         def x_quant(b):
@@ -138,14 +141,20 @@ def tile_full_tmix_params_pb_kernel(tc, x, x_v, W_v, v_hid, v2, v0, v_first, out
             for b in range(NB):
                 nc.tensor.transpose(bank[:, P * b:P * b + P], vh_sb[:, b, :], ident_b[:])
             nc.scalar.copy(out=vhT[:], in_=bank[:])
+            vbank = tp_pool.tile([P, P], BF16, name="vbank", tag="tp")
+            nc.tensor.transpose(vbank[:], v0rows[:], ident_b[:])
+            nc.vector.tensor_copy(out=v0c[:], in_=vbank[:, 0:16])
 
         def gate(c):
             cols = slice(CW * c, CW * c + CW)
             for i in range(NB):
                 hp = tp_pool.tile([P, CW], F32, name="hp", tag="tp")
-                nc.tensor.matmul(out=hp[:], lhsT=vhT[:, P * i:P * i + P], rhs=v2_sb[:, cols], start=True, stop=True)
-                nc.vector.tensor_tensor(out=t1[(c, i)][:], in0=hp[:], in1=v0b[:, cols], op=ALU.add)
-                nc.scalar.activation(out=mix[(c, i)][:], in_=t1[(c, i)][:], func=ACT.Sigmoid)
+                nc.tensor.matmul(out=hp[:], lhsT=vhT[:, P * i:P * i + P], rhs=v2_sb[:, cols], start=True, stop=False)
+                for q in range(4):
+                    j = 4 * c + q
+                    nc.tensor.matmul(out=hp[:, P * q:P * q + P], lhsT=v0c[:, j:j + 1].to_broadcast([P, P]),
+                                     rhs=ident_f[:], is_transpose=True, start=False, stop=(q == 3))
+                nc.scalar.activation(out=mix[(c, i)][:], in_=hp[:], func=ACT.Sigmoid)
                 nc.gpsimd.tensor_tensor(out=t1[(c, i)][:], in0=vf_sb[c][:, i, :], in1=mix[(c, i)][:], op=ALU.mult)
 
         wgs = {}
@@ -192,7 +201,7 @@ def tile_full_tmix_params_pb_kernel(tc, x, x_v, W_v, v_hid, v2, v0, v_first, out
             pt = p_pool.tile([P, CW], F32, name="pt")
             nc.vector.scalar_tensor_tensor(out=pt[:], in0=mix[(c, i)][:], scalar=1.0, in1=accs[(c, i)][:],
                                            op0=ALU.subtract, op1=ALU.mult)
-            nc.gpsimd.tensor_tensor(out=t1[(c, i)][:], in0=t1[(c, i)][:], in1=pt[:], op=ALU.subtract)
+            nc.vector.tensor_tensor(out=t1[(c, i)][:], in0=t1[(c, i)][:], in1=pt[:], op=ALU.subtract)
             nc.sync.dma_start(out=out[i, :, CW * c:CW * c + CW], in_=t1[(c, i)][:])
 
         x_transposes(0)

@@ -1,8 +1,6 @@
 from contextlib import ExitStack
 
-import concourse.bass as bass
 import concourse.mybir as mybir
-import concourse.tile as tile
 from concourse.masks import make_identity
 
 F32 = mybir.dt.float32
@@ -15,24 +13,29 @@ ACT = mybir.ActivationFunctionType
 
 P = 128
 NB = 4
+NT = NB * P
 C = 2048
 CO = 2048
 NG = 4
-UW = 256
-NU = CO // UW
 CW = 512
 NCH = CO // CW
 
-FLOPS = 2 * NB * P * C * CO + 2 * NB * P * 128 * CO
+FLOPS = 2 * NT * C * CO + 2 * NT * 128 * CO
+
+PINNED = True
+REG_ENG = "V"
+T1_ENG = "G"
 
 
 def tile_full_tmix_params_pb_kernel(tc, x, x_v, W_v, v_hid, v2, v0, v_first, out):
     nc = tc.nc
     with ExitStack() as ctx:
+        if PINNED:
+            ctx.enter_context(tc.manual_schedule())
         const = ctx.enter_context(tc.tile_pool(name="const", bufs=1))
-        wraw_pool = ctx.enter_context(tc.tile_pool(name="wraw", bufs=5))
-        wg_pool = ctx.enter_context(tc.tile_pool(name="wg", bufs=2))
-        wc_pool = ctx.enter_context(tc.tile_pool(name="wc", bufs=4))
+        wraw_pool = ctx.enter_context(tc.tile_pool(name="wraw", bufs=6))
+        wg_pool = ctx.enter_context(tc.tile_pool(name="wg", bufs=3))
+        wc_pool = ctx.enter_context(tc.tile_pool(name="wc", bufs=6))
         xw_pool = ctx.enter_context(tc.tile_pool(name="xw", bufs=2))
         vf_pool = ctx.enter_context(tc.tile_pool(name="vf", bufs=3))
         p_pool = ctx.enter_context(tc.tile_pool(name="pp", bufs=4))
@@ -43,101 +46,113 @@ def tile_full_tmix_params_pb_kernel(tc, x, x_v, W_v, v_hid, v2, v0, v_first, out
         make_identity(nc, ident_f[:])
         ident_b = const.tile([P, P], BF16, name="ident_b")
         make_identity(nc, ident_b[:])
+        v0rows = const.tile([P, P], BF16, name="v0rows")
+        nc.gpsimd.memset(v0rows[:], 0.0)
 
         a_bf = const.tile([P, 8, 2], BF16, name="a_bf")
         nc.scalar.dma_start(out=a_bf[:], in_=x_v.rearrange("a b c -> (a b c)").rearrange("(m p e) -> p m e", p=P, e=2))
 
-        x_sb = []
-        for b in range(NB):
-            xt = const.tile([P, C], BF16, name="x_sb%d" % b)
-            nc.sync.dma_start(out=xt[:], in_=x[b])
-            x_sb.append(xt)
-        vh_sb = const.tile([P, NB, P], BF16, name="vh_sb")
-        nc.sync.dma_start(out=vh_sb[:], in_=v_hid.rearrange("b t d -> t b d"))
-        v2_sb = const.tile([P, CO], BF16, name="v2_sb")
-        nc.sync.dma_start(out=v2_sb[:], in_=v2)
-        v0rows = const.tile([P, P], BF16, name="v0rows")
-        nc.gpsimd.memset(v0rows[:], 0.0)
-        nc.sync.dma_start(out=v0rows[0:16, :], in_=v0.rearrange("a b c -> (a b c)").rearrange("(j p) -> j p", p=P))
-        v0c = const.tile([P, 16], F32, name="v0c")
-
+        x_tbk = x.rearrange("b t k -> t b k")
         w_units = W_v.rearrange("(n r p) k -> n p r k", r=2, p=P)
         vf_chunks = v_first.rearrange("b t (c n) -> c t b n", n=CW)
-        wraw = []
-        vf_sb = []
-        for n in range(NU):
-            wr = wraw_pool.tile([P, 2, C], BF16, name="wr")
-            nc.sync.dma_start(out=wr[:], in_=w_units[n])
-            wraw.append(wr)
-            if n % 2 == 1:
-                vf = vf_pool.tile([P, NB, CW], BF16, name="vf")
-                nc.sync.dma_start(out=vf[:], in_=vf_chunks[n // 2])
-                vf_sb.append(vf)
+        xh = [const.tile([P, NB, C // 2], BF16, name="xh%d" % hf) for hf in range(2)]
+        vh_sb = const.tile([P, NB, P], BF16, name="vh_sb")
+        v2_sb = const.tile([P, CO], BF16, name="v2_sb")
+        wraw = {}
+        vf_sb = {}
+
+        def load_w(n):
+            wraw[n] = wraw_pool.tile([P, 2, C], BF16, name="wr")
+            nc.sync.dma_start(out=wraw[n][:], in_=w_units[n])
+
+        def load_vf(c):
+            vf_sb[c] = vf_pool.tile([P, NB, CW], BF16, name="vf")
+            nc.sync.dma_start(out=vf_sb[c][:], in_=vf_chunks[c])
+
+        nc.sync.dma_start(out=xh[0][:], in_=x_tbk[:, :, 0:C // 2])
+        nc.sync.dma_start(out=vh_sb[:], in_=v_hid.rearrange("b t d -> t b d"))
+        nc.sync.dma_start(out=v0rows[0:16, :], in_=v0.rearrange("a b c -> (a b c)").rearrange("(j p) -> j p", p=P))
+        nc.sync.dma_start(out=v2_sb[:], in_=v2)
+        load_w(0)
+        load_w(1)
+        nc.sync.dma_start(out=xh[1][:], in_=x_tbk[:, :, C // 2:C])
+        load_vf(0)
+        load_w(2)
+        load_w(3)
+        load_vf(1)
+        load_w(4)
+        load_w(5)
+        load_vf(2)
+        load_vf(3)
+        load_w(6)
+        load_w(7)
 
         a32 = const.tile([P, 16], F32, name="a32")
         nc.vector.tensor_copy(out=a32[:], in_=a_bf[:].rearrange("p m e -> p (m e)"))
         oma32 = const.tile([P, 16], F32, name="oma32")
         nc.vector.tensor_scalar(out=oma32[:], in0=a32[:], scalar1=-1.0, scalar2=1.0, op0=ALU.mult, op1=ALU.add)
 
-        xcodes = []
-        xscales = []
-        for b in range(NB):
-            xcodes.append(const.tile([P, NG * P], U32, name="xcodes%d" % b, align_bytes=64))
-            xscales.append(const.tile([P, NG * P], U8, name="xscales%d" % b, align_bytes=64))
+        xcodes = const.tile([P, NG, NT], U32, name="xcodes", align_bytes=64)
+        xscales = const.tile([P, NG, NT], U8, name="xscales", align_bytes=64)
         mix = {}
         t1 = {}
         for c in range(NCH):
             for i in range(NB):
                 mix[(c, i)] = const.tile([P, CW], F32, name="mix%d_%d" % (c, i))
                 t1[(c, i)] = const.tile([P, CW], F32, name="t1_%d_%d" % (c, i))
-        vhT = const.tile([P, NB * P], BF16, name="vhT")
+        vhT = const.tile([P, NT], BF16, name="vhT")
+        v0c = const.tile([P, 16], F32, name="v0c")
 
         xbanks = {}
+        y0s = {}
         xvps = {}
         xgs = {}
 
-        def x_transposes(b):
-            xwords = x_sb[b][:].bitcast(F32)
-            banks = []
-            for hb in range(2):
-                bank = tp_pool.tile([P, 512], F32, name="xbank", tag="tp")
-                for q in range(4):
-                    m = 4 * hb + q
-                    nc.tensor.transpose(bank[:, P * q:P * q + P], xwords[:, P * m:P * m + P], ident_f[:])
-                banks.append(bank)
-            xbanks[b] = banks
+        def x_transposes(j):
+            g, u = divmod(j, 2)
+            bank = tp_pool.tile([P, NT], F32, name="xbank", tag="tp")
+            lo = 256 * (g % 2) + P * u
+            for b in range(NB):
+                nc.tensor.transpose(bank[:, P * b:P * b + P], xh[g // 2][:, b, :].bitcast(F32)[:, lo:lo + P], ident_f[:])
+            xbanks[j] = bank
 
-        def x_mix(b):
-            y0 = xw_pool.tile([P, 16, P], F32, name="y0")
-            xvp = xw_pool.tile([P, 16, P], BF16, name="xvp")
-            for hb in range(2):
-                view = xbanks[b][hb][:].bitcast(BF16).rearrange("p (q s e) -> p q s e", q=4, e=2)
-                for q in range(4):
-                    for e in range(2):
-                        j = 8 * hb + 2 * q + e
-                        nc.scalar.activation(out=y0[:, j, :], in_=view[:, q, :, e], func=ACT.Copy,
-                                             scale=oma32[:, j:j + 1])
-                for q in range(4):
-                    for e in range(2):
-                        j = 8 * hb + 2 * q + e
-                        nc.vector.scalar_tensor_tensor(out=xvp[:, j, 1:P], in0=view[:, q, 0:P - 1, e],
-                                                       scalar=a32[:, j:j + 1], in1=y0[:, j, 1:P],
-                                                       op0=ALU.mult, op1=ALU.add)
-            nc.vector.tensor_copy(out=xvp[:, :, 0:1], in_=y0[:, :, 0:1])
-            xvps[b] = xvp
+        def x_scale(j):
+            g, u = divmod(j, 2)
+            if u == 0:
+                y0s[g] = xw_pool.tile([P, 4, NT], F32, name="y0")
+            view = xbanks[j][:].bitcast(BF16).rearrange("p (s e) -> p s e", e=2)
+            for e in range(2):
+                t = 2 * u + e
+                nc.scalar.activation(out=y0s[g][:, t, :], in_=view[:, :, e], func=ACT.Copy,
+                                     scale=oma32[:, 4 * g + t:4 * g + t + 1])
 
-        def x_regroup(b):
-            xg = xw_pool.tile([P, NG * P * 4], BF16, name="xg", align_bytes=64)
-            nc.gpsimd.tensor_scalar(out=xg[:].rearrange("p (g s t) -> p g s t", g=NG, t=4),
-                                    in0=xvps[b][:].rearrange("p (g t) s -> p g s t", t=4),
-                                    scalar1=1.0, scalar2=0.0, op0=ALU.mult, op1=ALU.add)
-            xgs[b] = xg
+        def x_add(j):
+            g, u = divmod(j, 2)
+            if u == 0:
+                xvps[g] = xw_pool.tile([P, 4, NT], BF16, name="xvp")
+            y0v = y0s[g][:].rearrange("p t (b s) -> p t b s", b=NB)
+            xvv = xvps[g][:].rearrange("p t (b s) -> p t b s", b=NB)
+            view = xbanks[j][:].bitcast(BF16).rearrange("p (b s e) -> p b s e", b=NB, e=2)
+            for e in range(2):
+                t = 2 * u + e
+                nc.vector.scalar_tensor_tensor(out=xvv[:, t, :, 1:P], in0=view[:, :, 0:P - 1, e],
+                                               scalar=a32[:, 4 * g + t:4 * g + t + 1], in1=y0v[:, t, :, 1:P],
+                                               op0=ALU.mult, op1=ALU.add)
 
-        def x_quant(b):
-            nc.vector.quantize_mx(out=xcodes[b][:].bitcast(FP8X4), scales=xscales[b][:], in_=xgs[b][:])
+        def x_regroup(g):
+            y0v = y0s[g][:].rearrange("p t (b s) -> p t b s", b=NB)
+            xvv = xvps[g][:].rearrange("p t (b s) -> p t b s", b=NB)
+            nc.vector.tensor_copy(out=xvv[:, :, :, 0], in_=y0v[:, :, :, 0])
+            xgs[g] = xw_pool.tile([P, NT * 4], BF16, name="xg", align_bytes=64)
+            dst = xgs[g][:].rearrange("p (c i t) -> p c t i", i=4, t=4)
+            src = xvps[g][:].rearrange("p t (c i) -> p c t i", i=4)
+            nc.vector.tensor_copy(out=dst, in_=src)
 
-        def vh_transposes():
-            bank = tp_pool.tile([P, NB * P], BF16, name="vhbank", tag="tp")
+        def x_quant(g):
+            nc.vector.quantize_mx(out=xcodes[:, g, :].bitcast(FP8X4), scales=xscales[:, g, :], in_=xgs[g][:])
+
+        def gate_setup():
+            bank = tp_pool.tile([P, NT], BF16, name="vhbank", tag="tp")
             for b in range(NB):
                 nc.tensor.transpose(bank[:, P * b:P * b + P], vh_sb[:, b, :], ident_b[:])
             nc.scalar.copy(out=vhT[:], in_=bank[:])
@@ -145,109 +160,125 @@ def tile_full_tmix_params_pb_kernel(tc, x, x_v, W_v, v_hid, v2, v0, v_first, out
             nc.tensor.transpose(vbank[:], v0rows[:], ident_b[:])
             nc.vector.tensor_copy(out=v0c[:], in_=vbank[:, 0:16])
 
-        def gate(c):
-            cols = slice(CW * c, CW * c + CW)
-            for i in range(NB):
-                hp = tp_pool.tile([P, CW], F32, name="hp", tag="tp")
-                nc.tensor.matmul(out=hp[:], lhsT=vhT[:, P * i:P * i + P], rhs=v2_sb[:, cols], start=True, stop=False)
-                for q in range(4):
-                    j = 4 * c + q
-                    nc.tensor.matmul(out=hp[:, P * q:P * q + P], lhsT=v0c[:, j:j + 1].to_broadcast([P, P]),
-                                     rhs=ident_f[:], is_transpose=True, start=False, stop=(q == 3))
-                nc.scalar.activation(out=mix[(c, i)][:], in_=hp[:], func=ACT.Sigmoid)
-                nc.gpsimd.tensor_tensor(out=t1[(c, i)][:], in0=vf_sb[c][:, i, :], in1=mix[(c, i)][:], op=ALU.mult)
+        hps = {}
 
+        def gate_mm(k):
+            c, i = divmod(k, NB)
+            hp = tp_pool.tile([P, CW], F32, name="hp", tag="tp")
+            nc.tensor.matmul(out=hp[:], lhsT=vhT[:, P * i:P * i + P], rhs=v2_sb[:, CW * c:CW * c + CW],
+                             start=True, stop=False)
+            for q in range(4):
+                jj = 4 * c + q
+                nc.tensor.matmul(out=hp[:, P * q:P * q + P], lhsT=v0c[:, jj:jj + 1].to_broadcast([P, P]),
+                                 rhs=ident_f[:], is_transpose=True, start=False, stop=(q == 3))
+            hps[k] = hp
+
+        def gate_sig(k):
+            nc.scalar.activation(out=mix[divmod(k, NB)][:], in_=hps[k][:], func=ACT.Sigmoid)
+
+        def first_term(k):
+            c, i = divmod(k, NB)
+            nc.gpsimd.tensor_tensor(out=t1[(c, i)][:], in0=vf_sb[c][:, i, :], in1=mix[(c, i)][:], op=ALU.mult)
+
+        wbanks = {}
         wgs = {}
         wcs = {}
 
-        def w_transposes(n):
-            wg = wg_pool.tile([P, NG * UW * 4], BF16, name="wg", align_bytes=64)
-            wgw = wg[:].bitcast(F32)
-            for g in range(NG):
-                bank = tp_pool.tile([P, 512], F32, name="wbank", tag="tp")
-                for u in range(2):
-                    for r in range(2):
-                        nc.tensor.transpose(bank[:, UW * u + P * r:UW * u + P * r + P],
-                                            wraw[n][:, r, :].bitcast(F32)[:, 256 * g + P * u:256 * g + P * u + P],
-                                            ident_f[:])
-                nc.scalar.copy(out=wgw[:, 512 * g:512 * g + 512].rearrange("p (c u) -> p c u", u=2),
-                               in_=bank[:].rearrange("p (u c) -> p c u", u=2))
-            wgs[n] = wg
+        def w_transposes(b):
+            c, rest = divmod(b, 8)
+            g, h = divmod(rest, 2)
+            bank = tp_pool.tile([P, 512], F32, name="wbank", tag="tp")
+            for u in range(2):
+                for r in range(2):
+                    lo = 256 * g + P * u
+                    nc.tensor.transpose(bank[:, 256 * u + P * r:256 * u + P * r + P],
+                                        wraw[2 * c + h][:, r, :].bitcast(F32)[:, lo:lo + P], ident_f[:])
+            wbanks[b] = bank
 
-        def w_quant(n):
-            wc = wc_pool.tile([P, NG * UW], U32, name="wc", align_bytes=64)
-            ws = wc_pool.tile([P, NG * UW], U8, name="ws", align_bytes=64)
-            nc.vector.quantize_mx(out=wc[:].bitcast(FP8X4), scales=ws[:], in_=wgs[n][:])
-            wcs[n] = (wc, ws)
+        def w_copy(b):
+            k, h = divmod(b, 2)
+            if h == 0:
+                wgs[k] = wg_pool.tile([P, CW * 4], BF16, name="wg", align_bytes=64)
+            nc.scalar.copy(out=wgs[k][:].bitcast(F32)[:, 512 * h:512 * h + 512].rearrange("p (c u) -> p c u", u=2),
+                           in_=wbanks[b][:].rearrange("p (u c) -> p c u", u=2))
+
+        def w_quant(k):
+            wc = wc_pool.tile([P, CW], U32, name="wc", align_bytes=64)
+            ws = wc_pool.tile([P, CW], U8, name="ws", align_bytes=64)
+            nc.vector.quantize_mx(out=wc[:].bitcast(FP8X4), scales=ws[:], in_=wgs[k][:])
+            wcs[k] = (wc, ws)
 
         accs = {}
 
-        def mx(n, i):
-            c = n // 2
-            h = n % 2
-            if h == 0:
-                accs[(c, i)] = acc_pool.tile([P, CW], F32, name="acc", tag="acc")
-            acc = accs[(c, i)]
-            wc, ws = wcs[n]
-            for g in range(NG):
-                nc.tensor.matmul_mx(out=acc[:, UW * h:UW * h + UW],
-                                    lhsT=xcodes[i][:, P * g:P * g + P].bitcast(FP8X4),
-                                    lhsT_scale=xscales[i][:, P * g:P * g + P],
-                                    rhs=wc[:, UW * g:UW * g + UW].bitcast(FP8X4),
-                                    rhs_scale=ws[:, UW * g:UW * g + UW],
+        def mx(k):
+            c, g = divmod(k, NG)
+            wc, ws = wcs[k]
+            for i in range(NB):
+                if g == 0:
+                    accs[(c, i)] = acc_pool.tile([P, CW], F32, name="acc", tag="acc")
+                nc.tensor.matmul_mx(out=accs[(c, i)][:],
+                                    lhsT=xcodes[:, g, P * i:P * i + P].bitcast(FP8X4),
+                                    lhsT_scale=xscales[:, g, P * i:P * i + P],
+                                    rhs=wc[:].bitcast(FP8X4), rhs_scale=ws[:],
                                     start=(g == 0), stop=(g == NG - 1))
 
-        def epilogue(c, i):
-            pt = p_pool.tile([P, CW], F32, name="pt")
-            nc.vector.scalar_tensor_tensor(out=pt[:], in0=mix[(c, i)][:], scalar=1.0, in1=accs[(c, i)][:],
+        pts = {}
+
+        def second_term(c, i):
+            pts[(c, i)] = p_pool.tile([P, CW], F32, name="pt")
+            nc.vector.scalar_tensor_tensor(out=pts[(c, i)][:], in0=mix[(c, i)][:], scalar=1.0, in1=accs[(c, i)][:],
                                            op0=ALU.subtract, op1=ALU.mult)
-            nc.vector.tensor_tensor(out=t1[(c, i)][:], in0=t1[(c, i)][:], in1=pt[:], op=ALU.subtract)
+
+        def finish(c, i):
+            nc.vector.tensor_tensor(out=t1[(c, i)][:], in0=t1[(c, i)][:], in1=pts[(c, i)][:], op=ALU.subtract)
             nc.sync.dma_start(out=out[i, :, CW * c:CW * c + CW], in_=t1[(c, i)][:])
 
         x_transposes(0)
-        vh_transposes()
-        x_mix(0)
-        x_transposes(1)
-        x_regroup(0)
-        x_mix(1)
-        x_quant(0)
-        x_transposes(2)
-        x_regroup(1)
-        gate(0)
-        w_transposes(0)
-        x_mix(2)
-        x_quant(1)
-        x_transposes(3)
-        x_regroup(2)
-        w_quant(0)
-        mx(0, 0)
-        mx(0, 1)
-        w_transposes(1)
-        x_mix(3)
-        x_quant(2)
-        x_regroup(3)
-        w_quant(1)
-        x_quant(3)
-        mx(1, 0)
-        mx(1, 1)
-        epilogue(0, 0)
-        epilogue(0, 1)
-        mx(0, 2)
-        mx(1, 2)
-        epilogue(0, 2)
-        w_transposes(2)
-        mx(0, 3)
-        mx(1, 3)
-        epilogue(0, 3)
-        for c in range(1, NCH):
-            gate(c)
-            w_quant(2 * c)
-            w_transposes(2 * c + 1)
-            for i in range(NB):
-                mx(2 * c, i)
-            w_quant(2 * c + 1)
-            if c + 1 < NCH:
-                w_transposes(2 * c + 2)
-            for i in range(NB):
-                mx(2 * c + 1, i)
-                epilogue(c, i)
+        gate_setup()
+        for j in range(14):
+            g, u = divmod(j, 2)
+            b = j - 2
+            if j < 8:
+                x_scale(j)
+                gate_mm(2 * j)
+                gate_mm(2 * j + 1)
+                x_add(j)
+                gate_sig(2 * j)
+            if 0 <= b < 8:
+                w_transposes(b)
+            if j < 8:
+                gate_sig(2 * j + 1)
+            if j < 7:
+                x_transposes(j + 1)
+            if 0 <= b < 8:
+                w_copy(b)
+            if j < 8 and u == 1:
+                x_regroup(g)
+            if u == 0 and 1 <= g <= 4:
+                x_quant(g - 1)
+            if 0 <= b < 8 and b % 2 == 1:
+                w_quant(b // 2)
+            if b - 2 >= 0 and (b - 2) % 2 == 1 and (b - 2) // 2 < 4:
+                mx((b - 2) // 2)
+            if 2 <= j < 10:
+                first_term(2 * (j - 2))
+                first_term(2 * (j - 2) + 1)
+        nbank = 8
+        nquant = 4
+        for k in range(4, 20):
+            c, g = divmod(k, NG)
+            if g == 0:
+                for i in range(NB):
+                    second_term(c - 1, i)
+            while nbank < 32 and nbank < 2 * (k + 3):
+                w_transposes(nbank)
+                w_transposes(nbank + 1)
+                w_copy(nbank)
+                w_copy(nbank + 1)
+                nbank += 2
+            while nquant < 16 and nquant <= k + 1:
+                w_quant(nquant)
+                nquant += 1
+            if k < 16:
+                mx(k)
+            finish(c - 1, g)

@@ -55,7 +55,7 @@ def tile_full_tmix_params_pb_kernel(tc, x, x_v, W_v, v_hid, v2, v0, v_first, out
         x_tbk = x.rearrange("b t k -> t b k")
         w_units = W_v.rearrange("(n r p) k -> n p r k", r=2, p=P)
         vf_chunks = v_first.rearrange("b t (c n) -> c t b n", n=CW)
-        xh = [const.tile([P, NB, C // 2], BF16, name="xh%d" % hf) for hf in range(2)]
+        xp = [const.tile([P, NB, C // NG], BF16, name="xp%d" % g) for g in range(NG)]
         vh_sb = const.tile([P, NB, P], BF16, name="vh_sb")
         v2_sb = const.tile([P, CO], BF16, name="v2_sb")
         wraw = {}
@@ -69,13 +69,18 @@ def tile_full_tmix_params_pb_kernel(tc, x, x_v, W_v, v_hid, v2, v0, v_first, out
             vf_sb[c] = vf_pool.tile([P, NB, CW], BF16, name="vf")
             nc.sync.dma_start(out=vf_sb[c][:], in_=vf_chunks[c])
 
-        nc.sync.dma_start(out=xh[0][:], in_=x_tbk[:, :, 0:C // 2])
+        def load_x(g):
+            nc.sync.dma_start(out=xp[g][:], in_=x_tbk[:, :, 512 * g:512 * g + 512])
+
+        load_x(0)
         nc.sync.dma_start(out=vh_sb[:], in_=v_hid.rearrange("b t d -> t b d"))
         nc.sync.dma_start(out=v0rows[0:16, :], in_=v0.rearrange("a b c -> (a b c)").rearrange("(j p) -> j p", p=P))
         nc.sync.dma_start(out=v2_sb[:], in_=v2)
+        load_x(1)
         load_w(0)
         load_w(1)
-        nc.sync.dma_start(out=xh[1][:], in_=x_tbk[:, :, C // 2:C])
+        load_x(2)
+        load_x(3)
         load_vf(0)
         load_w(2)
         load_w(3)
@@ -111,9 +116,8 @@ def tile_full_tmix_params_pb_kernel(tc, x, x_v, W_v, v_hid, v2, v0, v_first, out
         def x_transposes(j):
             g, u = divmod(j, 2)
             bank = tp_pool.tile([P, NT], F32, name="xbank", tag="tp")
-            lo = 256 * (g % 2) + P * u
             for b in range(NB):
-                nc.tensor.transpose(bank[:, P * b:P * b + P], xh[g // 2][:, b, :].bitcast(F32)[:, lo:lo + P], ident_f[:])
+                nc.tensor.transpose(bank[:, P * b:P * b + P], xp[g][:, b, :].bitcast(F32)[:, P * u:P * u + P], ident_f[:])
             xbanks[j] = bank
 
         def x_scale(j):
@@ -176,9 +180,9 @@ def tile_full_tmix_params_pb_kernel(tc, x, x_v, W_v, v_hid, v2, v0, v_first, out
         def gate_sig(k):
             nc.scalar.activation(out=mix[divmod(k, NB)][:], in_=hps[k][:], func=ACT.Sigmoid)
 
-        def first_term(k):
+        def first_term(k, eng):
             c, i = divmod(k, NB)
-            nc.gpsimd.tensor_tensor(out=t1[(c, i)][:], in0=vf_sb[c][:, i, :], in1=mix[(c, i)][:], op=ALU.mult)
+            eng.tensor_tensor(out=t1[(c, i)][:], in0=vf_sb[c][:, i, :], in1=mix[(c, i)][:], op=ALU.mult)
 
         wbanks = {}
         wgs = {}
@@ -229,8 +233,8 @@ def tile_full_tmix_params_pb_kernel(tc, x, x_v, W_v, v_hid, v2, v0, v_first, out
             nc.vector.scalar_tensor_tensor(out=pts[(c, i)][:], in0=mix[(c, i)][:], scalar=1.0, in1=accs[(c, i)][:],
                                            op0=ALU.subtract, op1=ALU.mult)
 
-        def finish(c, i):
-            nc.vector.tensor_tensor(out=t1[(c, i)][:], in0=t1[(c, i)][:], in1=pts[(c, i)][:], op=ALU.subtract)
+        def finish(c, i, eng):
+            eng.tensor_tensor(out=t1[(c, i)][:], in0=t1[(c, i)][:], in1=pts[(c, i)][:], op=ALU.subtract)
             nc.sync.dma_start(out=out[i, :, CW * c:CW * c + CW], in_=t1[(c, i)][:])
 
         x_transposes(0)
@@ -240,14 +244,11 @@ def tile_full_tmix_params_pb_kernel(tc, x, x_v, W_v, v_hid, v2, v0, v_first, out
             b = j - 2
             if j < 8:
                 x_scale(j)
-                gate_mm(2 * j)
-                gate_mm(2 * j + 1)
+                gate_mm(j)
                 x_add(j)
-                gate_sig(2 * j)
+                gate_sig(j)
             if 0 <= b < 8:
                 w_transposes(b)
-            if j < 8:
-                gate_sig(2 * j + 1)
             if j < 7:
                 x_transposes(j + 1)
             if 0 <= b < 8:
@@ -260,9 +261,8 @@ def tile_full_tmix_params_pb_kernel(tc, x, x_v, W_v, v_hid, v2, v0, v_first, out
                 w_quant(b // 2)
             if b - 2 >= 0 and (b - 2) % 2 == 1 and (b - 2) // 2 < 4:
                 mx((b - 2) // 2)
-            if 2 <= j < 10:
-                first_term(2 * (j - 2))
-                first_term(2 * (j - 2) + 1)
+            if 1 <= j < 9:
+                first_term(j - 1, nc.gpsimd)
         nbank = 8
         nquant = 4
         for k in range(4, 20):
@@ -276,9 +276,14 @@ def tile_full_tmix_params_pb_kernel(tc, x, x_v, W_v, v_hid, v2, v0, v_first, out
                 w_copy(nbank)
                 w_copy(nbank + 1)
                 nbank += 2
+            if k < 12:
+                gate_mm(k + 4)
+                gate_sig(k + 4)
             while nquant < 16 and nquant <= k + 1:
                 w_quant(nquant)
                 nquant += 1
             if k < 16:
                 mx(k)
-            finish(c - 1, g)
+            if 5 <= k < 13:
+                first_term(k + 3, nc.vector)
+            finish(c - 1, g, nc.gpsimd if (c == NCH and g < 2) else nc.vector)

@@ -214,10 +214,11 @@ def tile_full_tmix_params_pb_kernel(tc, x, x_v, W_v, v_hid, v2, v0, v_first, out
 
         accs = {}
 
-        def mx(k):
-            c, g = divmod(k, NG)
-            wc, ws = wcs[k]
-            for i in range(NB):
+        def mx(s):
+            todo = sorted([((s - i) % NG, i) for i in range(NB) if 0 <= s - i < 16], reverse=True)
+            for g, i in todo:
+                c = (s - i) // NG
+                wc, ws = wcs[s - i]
                 if g == 0:
                     accs[(c, i)] = acc_pool.tile([P, CW], F32, name="acc", tag="acc")
                 nc.tensor.matmul_mx(out=accs[(c, i)][:],
@@ -263,27 +264,26 @@ def tile_full_tmix_params_pb_kernel(tc, x, x_v, W_v, v_hid, v2, v0, v_first, out
                 mx((b - 2) // 2)
             if 1 <= j < 9:
                 first_term(j - 1, nc.gpsimd)
+        second_term(0, 0)
         nbank = 8
         nquant = 4
-        for k in range(4, 20):
-            c, g = divmod(k, NG)
-            if g == 0:
-                for i in range(NB):
-                    second_term(c - 1, i)
-            while nbank < 32 and nbank < 2 * (k + 3):
+        for s in range(4, 20):
+            while nbank < 32 and nbank < 2 * (s + 3):
                 w_transposes(nbank)
                 w_transposes(nbank + 1)
                 w_copy(nbank)
                 w_copy(nbank + 1)
                 nbank += 2
-            if k < 12:
-                gate_mm(k + 4)
-                gate_sig(k + 4)
-            while nquant < 16 and nquant <= k + 1:
+            if s < 12:
+                gate_mm(s + 4)
+                gate_sig(s + 4)
+            while nquant < 16 and nquant <= s + 1:
                 w_quant(nquant)
                 nquant += 1
-            if k < 16:
-                mx(k)
-            if 5 <= k < 13:
-                first_term(k + 3, nc.vector)
-            finish(c - 1, g, nc.gpsimd if (c == NCH and g < 2) else nc.vector)
+            if s < 19:
+                mx(s)
+            if 5 <= s < 13:
+                first_term(s + 3, nc.vector)
+            if s < 19:
+                second_term((s - 3) // NB, (s - 3) % NB)
+            finish((s - 4) // NB, (s - 4) % NB, nc.vector)

@@ -52,6 +52,9 @@ def tile_full_tmix_params_pb_kernel(tc, x, x_v, W_v, v_hid, v2, v0, v_first, out
         a_bf = const.tile([P, 8, 2], BF16, name="a_bf")
         nc.scalar.dma_start(out=a_bf[:], in_=x_v.rearrange("a b c -> (a b c)").rearrange("(m p e) -> p m e", p=P, e=2))
 
+        warm = const.tile([P, 1], F32, name="warm")
+        nc.scalar.activation(out=warm[:], in_=ident_f[:, 0:1], func=ACT.Sigmoid)
+
         x_tbk = x.rearrange("b t k -> t b k")
         w_units = W_v.rearrange("(n r p) k -> n p r k", r=2, p=P)
         vf_chunks = v_first.rearrange("b t (c n) -> c t b n", n=CW)
@@ -267,23 +270,26 @@ def tile_full_tmix_params_pb_kernel(tc, x, x_v, W_v, v_hid, v2, v0, v_first, out
         second_term(0, 0)
         nbank = 8
         nquant = 4
-        for s in range(4, 20):
-            while nbank < 32 and nbank < 2 * (s + 3):
-                w_transposes(nbank)
-                w_transposes(nbank + 1)
-                w_copy(nbank)
-                w_copy(nbank + 1)
-                nbank += 2
-            if s < 12:
-                gate_mm(s + 4)
-                gate_sig(s + 4)
-            while nquant < 16 and nquant <= s + 1:
+        for s0 in range(4, 20, 2):
+            while nbank < 32 and nbank < 2 * (s0 + 4):
+                for q in range(4):
+                    w_transposes(nbank + q)
+                for q in range(4):
+                    w_copy(nbank + q)
+                nbank += 4
+            for s in (s0, s0 + 1):
+                if s < 12:
+                    gate_mm(s + 4)
+                    gate_sig(s + 4)
+            while nquant < 16 and nquant <= s0 + 2:
                 w_quant(nquant)
                 nquant += 1
-            if s < 19:
-                mx(s)
-            if 5 <= s < 13:
-                first_term(s + 3, nc.vector)
-            if s < 19:
-                second_term((s - 3) // NB, (s - 3) % NB)
-            finish((s - 4) // NB, (s - 4) % NB, nc.vector)
+            for s in (s0, s0 + 1):
+                if s < 19:
+                    mx(s)
+            for s in (s0, s0 + 1):
+                if 5 <= s < 13:
+                    first_term(s + 3, nc.vector)
+                if s < 19:
+                    second_term((s - 3) // NB, (s - 3) % NB)
+                finish((s - 4) // NB, (s - 4) % NB, nc.vector)

@@ -53,7 +53,8 @@ def tile_full_tmix_params_pb_kernel(tc, x, x_v, W_v, v_hid, v2, v0, v_first, out
         nc.scalar.dma_start(out=a_bf[:], in_=x_v.rearrange("a b c -> (a b c)").rearrange("(m p e) -> p m e", p=P, e=2))
 
         warm = const.tile([P, 1], F32, name="warm")
-        nc.scalar.activation(out=warm[:], in_=ident_f[:, 0:1], func=ACT.Sigmoid)
+        nc.vector.memset(warm[:], 0.0)
+        nc.scalar.activation(out=warm[:], in_=warm[:], func=ACT.Sigmoid)
 
         x_tbk = x.rearrange("b t k -> t b k")
         w_units = W_v.rearrange("(n r p) k -> n p r k", r=2, p=P)
@@ -243,7 +244,7 @@ def tile_full_tmix_params_pb_kernel(tc, x, x_v, W_v, v_hid, v2, v0, v_first, out
 
         x_transposes(0)
         gate_setup()
-        for j in range(14):
+        for j in range(10):
             g, u = divmod(j, 2)
             b = j - 2
             if j < 8:
@@ -263,33 +264,30 @@ def tile_full_tmix_params_pb_kernel(tc, x, x_v, W_v, v_hid, v2, v0, v_first, out
                 x_quant(g - 1)
             if 0 <= b < 8 and b % 2 == 1:
                 w_quant(b // 2)
-            if b - 2 >= 0 and (b - 2) % 2 == 1 and (b - 2) // 2 < 4:
+            if b - 2 >= 0 and (b - 2) % 2 == 1 and (b - 2) // 2 < 2:
                 mx((b - 2) // 2)
             if 1 <= j < 9:
                 first_term(j - 1, nc.gpsimd)
-        second_term(0, 0)
         nbank = 8
         nquant = 4
-        for s0 in range(4, 20, 2):
-            while nbank < 32 and nbank < 2 * (s0 + 4):
-                for q in range(4):
-                    w_transposes(nbank + q)
-                for q in range(4):
-                    w_copy(nbank + q)
-                nbank += 4
-            for s in (s0, s0 + 1):
-                if s < 12:
-                    gate_mm(s + 4)
-                    gate_sig(s + 4)
-            while nquant < 16 and nquant <= s0 + 2:
+        for s in range(2, 20):
+            while nbank < 32 and nbank < 2 * (s + 3):
+                w_transposes(nbank)
+                w_transposes(nbank + 1)
+                w_copy(nbank)
+                w_copy(nbank + 1)
+                nbank += 2
+            if 4 <= s < 12:
+                gate_mm(s + 4)
+                gate_sig(s + 4)
+            while nquant < 16 and nquant <= s + 1:
                 w_quant(nquant)
                 nquant += 1
-            for s in (s0, s0 + 1):
-                if s < 19:
-                    mx(s)
-            for s in (s0, s0 + 1):
-                if 5 <= s < 13:
-                    first_term(s + 3, nc.vector)
-                if s < 19:
-                    second_term((s - 3) // NB, (s - 3) % NB)
+            if s < 19:
+                mx(s)
+            if 5 <= s < 13:
+                first_term(s + 3, nc.vector)
+            if 3 <= s < 19:
+                second_term((s - 3) // NB, (s - 3) % NB)
+            if s >= 4:
                 finish((s - 4) // NB, (s - 4) % NB, nc.vector)

@@ -252,6 +252,8 @@ def tile_full_tmix_params_pb_kernel(tc, x, x_v, W_v, v_hid, v2, v0, v_first, out
                 gate_mm(j)
                 x_add(j)
                 gate_sig(j)
+                gate_mm(8 + j)
+                gate_sig(8 + j)
             if 0 <= b < 8:
                 w_transposes(b)
             if j < 7:
@@ -277,9 +279,6 @@ def tile_full_tmix_params_pb_kernel(tc, x, x_v, W_v, v_hid, v2, v0, v_first, out
                 w_copy(nbank)
                 w_copy(nbank + 1)
                 nbank += 2
-            if 4 <= s < 12:
-                gate_mm(s + 4)
-                gate_sig(s + 4)
             while nquant < 16 and nquant <= s + 1:
                 w_quant(nquant)
                 nquant += 1

from contextlib import ExitStack

import concourse.mybir as mybir
from concourse.masks import make_identity

F32 = mybir.dt.float32
BF16 = mybir.dt.bfloat16
U32 = mybir.dt.uint32
U8 = mybir.dt.uint8
FP8X4 = mybir.dt.float8_e4m3fn_x4
ALU = mybir.AluOpType
ACT = mybir.ActivationFunctionType

P = 128
NB = 4
NT = NB * P
C = 2048
CO = 2048
NG = 4
CW = 512
NCH = CO // CW

FLOPS = 2 * NT * C * CO + 2 * NT * 128 * CO

PINNED = True
REG_ENG = "V"
T1_ENG = "G"


def tile_full_tmix_params_pb_kernel(tc, x, x_v, W_v, v_hid, v2, v0, v_first, out):
    nc = tc.nc
    with ExitStack() as ctx:
        if PINNED:
            ctx.enter_context(tc.manual_schedule())
        const = ctx.enter_context(tc.tile_pool(name="const", bufs=1))
        wraw_pool = ctx.enter_context(tc.tile_pool(name="wraw", bufs=6))
        wg_pool = ctx.enter_context(tc.tile_pool(name="wg", bufs=3))
        wc_pool = ctx.enter_context(tc.tile_pool(name="wc", bufs=6))
        xw_pool = ctx.enter_context(tc.tile_pool(name="xw", bufs=2))
        vf_pool = ctx.enter_context(tc.tile_pool(name="vf", bufs=3))
        p_pool = ctx.enter_context(tc.tile_pool(name="pp", bufs=4))
        acc_pool = ctx.enter_context(tc.psum_pool(name="acc", bufs=4))
        tp_pool = ctx.enter_context(tc.psum_pool(name="tp", bufs=4))

        ident_f = const.tile([P, P], F32, name="ident_f")
        make_identity(nc, ident_f[:])
        ident_b = const.tile([P, P], BF16, name="ident_b")
        make_identity(nc, ident_b[:])
        v0rows = const.tile([P, P], BF16, name="v0rows")
        nc.gpsimd.memset(v0rows[:], 0.0)

        a_bf = const.tile([P, 8, 2], BF16, name="a_bf")
        nc.scalar.dma_start(out=a_bf[:], in_=x_v.rearrange("a b c -> (a b c)").rearrange("(m p e) -> p m e", p=P, e=2))

        warm = const.tile([P, 1], F32, name="warm")
        nc.vector.memset(warm[:], 0.0)
        nc.scalar.activation(out=warm[:], in_=warm[:], func=ACT.Sigmoid)

        x_tbk = x.rearrange("b t k -> t b k")
        w_units = W_v.rearrange("(n r p) k -> n p r k", r=2, p=P)
        vf_chunks = v_first.rearrange("b t (c n) -> c t b n", n=CW)
        xp = [const.tile([P, NB, C // NG], BF16, name="xp%d" % g) for g in range(NG)]
        vh_sb = const.tile([P, NB, P], BF16, name="vh_sb")
        v2_sb = const.tile([P, CO], BF16, name="v2_sb")
        wraw = {}
        vf_sb = {}

        def load_w(n):
            wraw[n] = wraw_pool.tile([P, 2, C], BF16, name="wr")
            nc.sync.dma_start(out=wraw[n][:], in_=w_units[n])

        def load_vf(c):
            vf_sb[c] = vf_pool.tile([P, NB, CW], BF16, name="vf")
            nc.sync.dma_start(out=vf_sb[c][:], in_=vf_chunks[c])

        def load_x(g):
            nc.sync.dma_start(out=xp[g][:], in_=x_tbk[:, :, 512 * g:512 * g + 512])

        load_x(0)
        nc.sync.dma_start(out=vh_sb[:], in_=v_hid.rearrange("b t d -> t b d"))
        nc.sync.dma_start(out=v0rows[0:16, :], in_=v0.rearrange("a b c -> (a b c)").rearrange("(j p) -> j p", p=P))
        nc.sync.dma_start(out=v2_sb[:], in_=v2)
        load_x(1)
        load_w(0)
        load_w(1)
        load_x(2)
        load_x(3)
        load_vf(0)
        load_w(2)
        load_w(3)
        load_vf(1)
        load_w(4)
        load_w(5)
        load_vf(2)
        load_vf(3)
        load_w(6)
        load_w(7)

        a32 = const.tile([P, 16], F32, name="a32")
        nc.vector.tensor_copy(out=a32[:], in_=a_bf[:].rearrange("p m e -> p (m e)"))
        oma32 = const.tile([P, 16], F32, name="oma32")
        nc.vector.tensor_scalar(out=oma32[:], in0=a32[:], scalar1=-1.0, scalar2=1.0, op0=ALU.mult, op1=ALU.add)

        xcodes = const.tile([P, NG, NT], U32, name="xcodes", align_bytes=64)
        xscales = const.tile([P, NG, NT], U8, name="xscales", align_bytes=64)
        mix = {}
        t1 = {}
        for c in range(NCH):
            for i in range(NB):
                mix[(c, i)] = const.tile([P, CW], F32, name="mix%d_%d" % (c, i))
                t1[(c, i)] = const.tile([P, CW], F32, name="t1_%d_%d" % (c, i))
        vhT = const.tile([P, NT], BF16, name="vhT")
        v0c = const.tile([P, 16], F32, name="v0c")

        xbanks = {}
        y0s = {}
        xvps = {}
        xgs = {}

        def x_transposes(j):
            g, u = divmod(j, 2)
            bank = tp_pool.tile([P, NT], F32, name="xbank", tag="tp")
            for b in range(NB):
                nc.tensor.transpose(bank[:, P * b:P * b + P], xp[g][:, b, :].bitcast(F32)[:, P * u:P * u + P], ident_f[:])
            xbanks[j] = bank

        def x_scale(j):
            g, u = divmod(j, 2)
            if u == 0:
                y0s[g] = xw_pool.tile([P, 4, NT], F32, name="y0")
            view = xbanks[j][:].bitcast(BF16).rearrange("p (s e) -> p s e", e=2)
            for e in range(2):
                t = 2 * u + e
                nc.scalar.activation(out=y0s[g][:, t, :], in_=view[:, :, e], func=ACT.Copy,
                                     scale=oma32[:, 4 * g + t:4 * g + t + 1])

        def x_add(j):
            g, u = divmod(j, 2)
            if u == 0:
                xvps[g] = xw_pool.tile([P, 4, NT], BF16, name="xvp")
            y0v = y0s[g][:].rearrange("p t (b s) -> p t b s", b=NB)
            xvv = xvps[g][:].rearrange("p t (b s) -> p t b s", b=NB)
            view = xbanks[j][:].bitcast(BF16).rearrange("p (b s e) -> p b s e", b=NB, e=2)
            for e in range(2):
                t = 2 * u + e
                nc.vector.scalar_tensor_tensor(out=xvv[:, t, :, 1:P], in0=view[:, :, 0:P - 1, e],
                                               scalar=a32[:, 4 * g + t:4 * g + t + 1], in1=y0v[:, t, :, 1:P],
                                               op0=ALU.mult, op1=ALU.add)

        def x_regroup(g):
            y0v = y0s[g][:].rearrange("p t (b s) -> p t b s", b=NB)
            xvv = xvps[g][:].rearrange("p t (b s) -> p t b s", b=NB)
            nc.vector.tensor_copy(out=xvv[:, :, :, 0], in_=y0v[:, :, :, 0])
            xgs[g] = xw_pool.tile([P, NT * 4], BF16, name="xg", align_bytes=64)
            dst = xgs[g][:].rearrange("p (c i t) -> p c t i", i=4, t=4)
            src = xvps[g][:].rearrange("p t (c i) -> p c t i", i=4)
            nc.vector.tensor_copy(out=dst, in_=src)

        def x_quant(g):
            nc.vector.quantize_mx(out=xcodes[:, g, :].bitcast(FP8X4), scales=xscales[:, g, :], in_=xgs[g][:])

        def gate_setup():
            bank = tp_pool.tile([P, NT], BF16, name="vhbank", tag="tp")
            for b in range(NB):
                nc.tensor.transpose(bank[:, P * b:P * b + P], vh_sb[:, b, :], ident_b[:])
            nc.scalar.copy(out=vhT[:], in_=bank[:])
            vbank = tp_pool.tile([P, P], BF16, name="vbank", tag="tp")
            nc.tensor.transpose(vbank[:], v0rows[:], ident_b[:])
            nc.vector.tensor_copy(out=v0c[:], in_=vbank[:, 0:16])

        hps = {}

        def gate_mm(k):
            c, i = divmod(k, NB)
            hp = tp_pool.tile([P, CW], F32, name="hp", tag="tp")
            nc.tensor.matmul(out=hp[:], lhsT=vhT[:, P * i:P * i + P], rhs=v2_sb[:, CW * c:CW * c + CW],
                             start=True, stop=False)
            for q in range(4):
                jj = 4 * c + q
                nc.tensor.matmul(out=hp[:, P * q:P * q + P], lhsT=v0c[:, jj:jj + 1].to_broadcast([P, P]),
                                 rhs=ident_f[:], is_transpose=True, start=False, stop=(q == 3))
            hps[k] = hp

        def gate_sig(k):
            nc.scalar.activation(out=mix[divmod(k, NB)][:], in_=hps[k][:], func=ACT.Sigmoid)

        def first_term(k, eng):
            c, i = divmod(k, NB)
            eng.tensor_tensor(out=t1[(c, i)][:], in0=vf_sb[c][:, i, :], in1=mix[(c, i)][:], op=ALU.mult)

        wbanks = {}
        wgs = {}
        wcs = {}

        def w_transposes(b):
            c, rest = divmod(b, 8)
            g, h = divmod(rest, 2)
            bank = tp_pool.tile([P, 512], F32, name="wbank", tag="tp")
            for u in range(2):
                for r in range(2):
                    lo = 256 * g + P * u
                    nc.tensor.transpose(bank[:, 256 * u + P * r:256 * u + P * r + P],
                                        wraw[2 * c + h][:, r, :].bitcast(F32)[:, lo:lo + P], ident_f[:])
            wbanks[b] = bank

        def w_copy(b):
            k, h = divmod(b, 2)
            if h == 0:
                wgs[k] = wg_pool.tile([P, CW * 4], BF16, name="wg", align_bytes=64)
            nc.scalar.copy(out=wgs[k][:].bitcast(F32)[:, 512 * h:512 * h + 512].rearrange("p (c u) -> p c u", u=2),
                           in_=wbanks[b][:].rearrange("p (u c) -> p c u", u=2))

        def w_quant(k):
            wc = wc_pool.tile([P, CW], U32, name="wc", align_bytes=64)
            ws = wc_pool.tile([P, CW], U8, name="ws", align_bytes=64)
            nc.vector.quantize_mx(out=wc[:].bitcast(FP8X4), scales=ws[:], in_=wgs[k][:])
            wcs[k] = (wc, ws)

        accs = {}

        def mx(s):
            todo = sorted([((s - i) % NG, i) for i in range(NB) if 0 <= s - i < 16], reverse=True)
            for g, i in todo:
                c = (s - i) // NG
                wc, ws = wcs[s - i]
                if g == 0:
                    accs[(c, i)] = acc_pool.tile([P, CW], F32, name="acc", tag="acc")
                nc.tensor.matmul_mx(out=accs[(c, i)][:],
                                    lhsT=xcodes[:, g, P * i:P * i + P].bitcast(FP8X4),
                                    lhsT_scale=xscales[:, g, P * i:P * i + P],
                                    rhs=wc[:].bitcast(FP8X4), rhs_scale=ws[:],
                                    start=(g == 0), stop=(g == NG - 1))

        pts = {}

        def second_term(c, i):
            pts[(c, i)] = p_pool.tile([P, CW], F32, name="pt")
            nc.vector.scalar_tensor_tensor(out=pts[(c, i)][:], in0=mix[(c, i)][:], scalar=1.0, in1=accs[(c, i)][:],
                                           op0=ALU.subtract, op1=ALU.mult)

        def finish(c, i, eng):
            eng.tensor_tensor(out=t1[(c, i)][:], in0=t1[(c, i)][:], in1=pts[(c, i)][:], op=ALU.subtract)
            nc.sync.dma_start(out=out[i, :, CW * c:CW * c + CW], in_=t1[(c, i)][:])

        x_transposes(0)
        gate_setup()
        for j in range(10):
            g, u = divmod(j, 2)
            b = j - 2
            if j < 8:
                x_scale(j)
                gate_mm(j)
                x_add(j)
                gate_sig(j)
                gate_mm(8 + j)
                gate_sig(8 + j)
            if 0 <= b < 8:
                w_transposes(b)
            if j < 7:
                x_transposes(j + 1)
            if 0 <= b < 8:
                w_copy(b)
            if j < 8 and u == 1:
                x_regroup(g)
            if u == 0 and 1 <= g <= 4:
                x_quant(g - 1)
            if 0 <= b < 8 and b % 2 == 1:
                w_quant(b // 2)
            if b - 2 >= 0 and (b - 2) % 2 == 1 and (b - 2) // 2 < 2:
                mx((b - 2) // 2)
            if 1 <= j < 9:
                first_term(j - 1, nc.gpsimd)
        nbank = 8
        nquant = 4
        for s in range(2, 20):
            while nbank < 32 and nbank < 2 * (s + 3):
                w_transposes(nbank)
                w_transposes(nbank + 1)
                w_copy(nbank)
                w_copy(nbank + 1)
                nbank += 2
            while nquant < 16 and nquant <= s + 1:
                w_quant(nquant)
                nquant += 1
            if s < 19:
                mx(s)
            if 5 <= s < 13:
                first_term(s + 3, nc.vector)
            if 3 <= s < 19:
                second_term((s - 3) // NB, (s - 3) % NB)
            if s >= 4:
                finish((s - 4) // NB, (s - 4) % NB, nc.vector)
